import numpy as np
import ml_dtypes


def mxq(x, axis, fmt="e4m3"):
    dtype, down = {"e4m3": (ml_dtypes.float8_e4m3fn, 7), "e5m2": (ml_dtypes.float8_e5m2, 14)}[fmt]
    v = np.moveaxis(np.asarray(x, np.float32).astype(ml_dtypes.bfloat16).astype(np.float64), axis, -1)
    blocks = v.reshape(v.shape[:-1] + (-1, 32))
    amax = np.abs(blocks).max(-1, keepdims=True)
    byte = np.maximum(np.where(amax > 0, np.frexp(amax)[1] - 1 + 127, 0) - down, 1)
    scale = np.exp2(byte - 127.0)
    codes = (blocks / scale).astype(np.float32).astype(dtype).astype(np.float64)
    return np.moveaxis((codes * scale).reshape(v.shape), -1, axis)


WIDE = False


def mx_kscale(k):
    if not WIDE:
        return np.ones(k)
    levels = np.array([10, -10, 5, -5, 0])
    a = np.random.permutation(np.resize(levels, k // 512 * 4)).reshape(k // 512, 4)
    idx = np.arange(k)
    return np.exp2(a[idx // 512, idx % 128 // 32])


BF16 = ml_dtypes.bfloat16


def bf(x):
    return np.asarray(x, np.float32).astype(BF16)


def f64(x):
    return np.asarray(x).astype(np.float64)


B, L, N, O = 2, 2, 1024, 512

LOOP = 1.0


def setup_inputs():
    s = mx_kscale(N)
    g = np.random.random((B, L, 1, N)) * 2.0
    mask = np.random.random((B, L, N, N)) * (4.0 / N) * g + np.eye(N) * np.random.random((B, L, N, 1)) * 2.0
    return {"x": bf(np.random.standard_normal((B, L, N, N)) * s),
            "mask": bf(mask),
            "weight": bf(np.random.standard_normal((N, O)) / np.sqrt(N) / s[:, None]),
            "bias": bf(np.random.standard_normal(O) * 0.3)}


def reference(x, mask, weight, bias):
    xf = f64(x).reshape(B * L, N, N)
    mf = f64(mask).reshape(B * L, N, N)
    eye = np.eye(N)
    m_sl = mf * (1.0 - eye) + LOOP * eye
    d = np.sum(m_sl, axis=1)
    inv_sqrt_d = 1.0 / np.sqrt(d)
    h = xf * inv_sqrt_d[:, :, None]
    out = np.maximum((mxq(h, 2, "e4m3") @ mxq(f64(weight), 0, "e4m3")) + f64(bias), 0.0)
    return out.reshape(B, L, N, O)

@@ -1,0 +1,310 @@
+from contextlib import ExitStack
+
+import concourse.mybir as mybir
+from concourse.masks import make_identity
+
+FP8X4 = mybir.dt.float8_e4m3fn_x4
+BF16 = mybir.dt.bfloat16
+F32 = mybir.dt.float32
+U32 = mybir.dt.uint32
+U8 = mybir.dt.uint8
+ALU = mybir.AluOpType
+ACT = mybir.ActivationFunctionType
+AX = mybir.AxisListType
+
+P = 128
+GRAPHS = 4
+NODES = 1024
+FEAT = 1024
+OUTF = 512
+XT = 8
+MC = 4
+MT = 2
+NK = 16
+ROUNDS = 16
+FLOPS = 2 * GRAPHS * NODES * FEAT * OUTF
+
+
+def tile_gcn_t_kernel(tc, x, mask, weight, bias, out):
+    nc = tc.nc
+    xg = x.rearrange("a b (p t) k -> (a b) p t k", t=XT)
+    mg = mask.rearrange("a b (c p t) i -> (a b) p c t i", c=MC, p=P, t=MT)
+    og = out.rearrange("a b (p t) o -> (a b) p t o", t=XT)
+    wv = weight.rearrange("(c t p) o -> p c t o", c=2, t=4, p=P)
+    bv = bias.rearrange("(r n) -> r n", r=1)
+
+    with ExitStack() as ctx:
+        const = ctx.enter_context(tc.tile_pool(name="const", bufs=1))
+        mpool = ctx.enter_context(tc.tile_pool(name="mpool", bufs=3))
+        xpool = ctx.enter_context(tc.tile_pool(name="xpool", bufs=3))
+        hpool = ctx.enter_context(tc.tile_pool(name="hpool", bufs=3))
+        gpool = ctx.enter_context(tc.tile_pool(name="gpool", bufs=3))
+        cpool = ctx.enter_context(tc.tile_pool(name="cpool", bufs=3))
+        small = ctx.enter_context(tc.tile_pool(name="small", bufs=2))
+        opool = ctx.enter_context(tc.tile_pool(name="opool", bufs=12))
+        psum_t = ctx.enter_context(tc.psum_pool(name="psum_t", bufs=3))
+        psum_o = ctx.enter_context(tc.psum_pool(name="psum_o", bufs=4))
+        psum_d = ctx.enter_context(tc.psum_pool(name="psum_d", bufs=1))
+        ctx.enter_context(tc.manual_schedule())
+
+        ident_f = const.tile([P, P], F32, name="ident_f")
+        make_identity(nc, ident_f[:])
+        one_col = const.tile([P, 1], F32, name="one_col")
+        nc.vector.memset(one_col[:], 1.0)
+        bias_row = const.tile([P, OUTF], BF16, name="bias_row")
+        nc.vector.memset(bias_row[:], 0.0)
+        nc.scalar.dma_start(out=bias_row[0:1, :], in_=bv)
+        warm = const.tile([P, 1], F32, name="warm")
+        nc.scalar.sqrt(out=warm[:], in_=one_col[:])
+        ones_b = const.tile([P, P], BF16, name="ones_b")
+        nc.vector.memset(ones_b[:], 1.0)
+        ident_b = const.tile([P, P], BF16, name="ident_b")
+        nc.vector.tensor_copy(out=ident_b[:], in_=ident_f[:])
+        e_sel = const.tile([P, 8], F32, name="e_sel")
+        nc.vector.tensor_reduce(
+            out=e_sel[:], in_=ident_f[:].rearrange("p (q t) -> p t q", t=8), axis=AX.X, op=ALU.add
+        )
+        g_sel = const.tile([P, 16], F32, name="g_sel")
+        nc.vector.tensor_reduce(
+            out=g_sel[:], in_=ident_f[:].rearrange("p (q t) -> p q t", t=8), axis=AX.X, op=ALU.add
+        )
+
+        mtiles = {}
+        xs = {}
+        rss = {}
+        dps = {}
+        hs = {}
+        xts = {}
+        grps = {}
+        cds = {}
+        ops = {}
+
+        def load_mask(g):
+            m = mpool.tile([P, MC, MT, NODES], BF16, name="m%d" % g, tag="m")
+            mtiles[g] = m
+            if g == 0:
+                for c in range(MC):
+                    nc.sync.dma_start(out=m[:, c], in_=mg[g][:, c])
+            else:
+                nc.sync.dma_start(out=m[:], in_=mg[g])
+
+        def self_loops(g):
+            m = mtiles[g]
+            w = P * MT
+            for c in range(MC):
+                for t in range(MT):
+                    region = m[:, c, t, c * w : (c + 1) * w]
+                    nc.gpsimd.affine_select(
+                        out=region,
+                        in_=region,
+                        pattern=[[-1, w]],
+                        compare_op=ALU.not_equal,
+                        fill=1.0,
+                        base=t,
+                        channel_multiplier=MT,
+                    )
+
+        def load_x(g, t0, t1):
+            if g not in xs:
+                xs[g] = xpool.tile([P, XT, FEAT], BF16, name="x%d" % g, tag="x")
+            nc.sync.dma_start(out=xs[g][:, t0:t1, :], in_=xg[g][:, t0:t1, :])
+
+        def col_sums(g):
+            m = mtiles[g]
+            d_ps = psum_d.tile([P, MC, 8, NK], F32, name="d_ps%d" % g, tag="d")
+            dps[g] = d_ps
+            for c in range(MC):
+                for ib in range(8):
+                    for t in range(MT):
+                        nc.tensor.matmul(
+                            out=d_ps[:, c, ib, :],
+                            lhsT=m[:, c, t, ib * P : (ib + 1) * P],
+                            rhs=ones_b[:, 0:NK],
+                            start=(t == 0),
+                            stop=(t == MT - 1),
+                        )
+
+        spread = {}
+
+        def degree_v(g):
+            d_sb = small.tile([P, 8], F32, name="d_sb%d" % g, tag="d_sb")
+            nc.vector.tensor_reduce(
+                out=d_sb[:],
+                in_=dps[g][:].rearrange("p c i n -> p i c n")[:, :, :, 0],
+                axis=AX.X,
+                op=ALU.add,
+            )
+            w_t = small.tile([P, 8, 16], F32, name="spread%d" % g, tag="spread")
+            nc.vector.tensor_tensor(
+                out=w_t[:],
+                in0=d_sb[:].unsqueeze(2).to_broadcast([P, 8, 16]),
+                in1=g_sel[:].unsqueeze(1).to_broadcast([P, 8, 16]),
+                op=ALU.mult,
+            )
+            spread[g] = w_t
+
+        def degree_pe(g):
+            nc.tensor.matmul(
+                out=dps[g][:, 0, 0, 0:8],
+                lhsT=spread[g][:].rearrange("p b q -> p (b q)"),
+                rhs=e_sel[:],
+                start=True,
+                stop=True,
+            )
+
+        sqs = {}
+
+        def degree_sqrt(g):
+            sq = small.tile([P, 8], F32, name="sq%d" % g, tag="sq")
+            nc.scalar.sqrt(out=sq[:], in_=dps[g][:, 0, 0, 0:8])
+            sqs[g] = sq
+
+        def degree_recip(g):
+            rs = small.tile([P, 8], F32, name="rs%d" % g, tag="rs")
+            nc.vector.reciprocal(out=rs[:], in_=sqs[g][:])
+            rss[g] = rs
+
+        def scale_rows(r):
+            g, q = divmod(r, 4)
+            h = hpool.tile([P, 2, FEAT], BF16, name="h%d" % r, tag="h")
+            hs[r] = h
+            for s in range(2):
+                t = 2 * q + s
+                nc.vector.tensor_scalar(
+                    out=h[:, s, :],
+                    in0=xs[g][:, t, :],
+                    scalar1=rss[g][:, t : t + 1],
+                    scalar2=None,
+                    op0=ALU.mult,
+                )
+
+        def transposes(r):
+            for s in range(2):
+                xt = psum_t.tile([P, 8, P], BF16, name="xt%d_%d" % (r, s), tag="xt")
+                xts[(r, s)] = xt
+                for kb in range(8):
+                    nc.tensor.transpose(xt[:, kb, :], hs[r][:, s, kb * P : (kb + 1) * P], ident_b[:])
+
+        def regroup(r):
+            grp = gpool.tile([P, 2, 2, P, 4], BF16, name="grp%d" % r, tag="grp", align_bytes=64)
+            grps[r] = grp
+            for s in range(2):
+                nc.scalar.copy(
+                    out=grp[:, s], in_=xts[(r, s)][:].rearrange("p (c t) i -> p c i t", c=2)
+                )
+
+        def quantise(r):
+            codes = cpool.tile([P, 4 * P], U32, name="codes%d" % r, tag="codes", align_bytes=64)
+            scl = cpool.tile([P, 4 * P], U8, name="scl%d" % r, tag="scl", align_bytes=64)
+            cds[r] = (codes, scl)
+            nc.vector.quantize_mx(
+                out=codes[:].bitcast(FP8X4),
+                scales=scl[:],
+                in_=grps[r][:].rearrange("p s c i t -> p (s c i t)"),
+            )
+
+        def products(r):
+            codes, scl = cds[r]
+            for s in range(2):
+                o_ps = psum_o.tile([P, OUTF], F32, name="o_ps%d_%d" % (r, s), tag="o")
+                ops[(r, s)] = o_ps
+                for c in range(2):
+                    cols = slice((2 * s + c) * P, (2 * s + c + 1) * P)
+                    nc.tensor.matmul_mx(
+                        out=o_ps[:],
+                        lhsT=codes[:, cols].bitcast(FP8X4),
+                        lhsT_scale=scl[:, cols],
+                        rhs=w_codes[:, c, :].bitcast(FP8X4),
+                        rhs_scale=w_scl[:, c, :],
+                        start=(c == 0),
+                        stop=(c == 1),
+                    )
+
+        def epilogue(r):
+            g, q = divmod(r, 4)
+            o_sb = opool.tile([P, 2, OUTF], F32, name="o_sb%d" % r, tag="o_sb")
+            for s in range(2):
+                nc.vector.tensor_tensor(
+                    out=o_sb[:, s, :], in0=ops[(r, s)][:], in1=bias_bc[:], op=ALU.add
+                )
+            nc.scalar.activation(out=o_sb[:, 0, :], in_=o_sb[:, 0, :], func=ACT.Relu)
+            nc.vector.tensor_scalar_max(out=o_sb[:, 1, :], in0=o_sb[:, 1, :], scalar1=0.0)
+            nc.sync.dma_start(out=og[g][:, 2 * q : 2 * q + 2, :], in_=o_sb[:])
+
+        load_mask(0)
+        load_x(0, 0, 2)
+        w_raw = const.tile([P, 2, 4, OUTF], BF16, name="w_raw")
+        nc.sync.dma_start(out=w_raw[:], in_=wv)
+        load_x(0, 2, 4)
+        load_x(0, 4, 8)
+        load_mask(1)
+        load_x(1, 0, 4)
+        load_x(1, 4, 8)
+        load_mask(2)
+        load_x(2, 0, 4)
+        load_x(2, 4, 8)
+        for g in range(3):
+            self_loops(g)
+
+        col_sums(0)
+        load_mask(3)
+        self_loops(3)
+        degree_v(0)
+        degree_pe(0)
+        degree_sqrt(0)
+        degree_recip(0)
+
+        w_grp = const.tile([P, 2, OUTF, 4], BF16, name="w_grp", align_bytes=64)
+        w_codes = const.tile([P, 2, OUTF], U32, name="w_codes", align_bytes=64)
+        w_scl = const.tile([P, 2, OUTF], U8, name="w_scl", align_bytes=64)
+
+        def weight_regroup(c):
+            nc.vector.tensor_copy(
+                out=w_grp[:, c].rearrange("p (a i) t -> p a t i", i=4),
+                in_=w_raw[:, c].rearrange("p t (a i) -> p a t i", i=4),
+            )
+
+        scale_rows(0)
+        transposes(0)
+        regroup(0)
+        weight_regroup(0)
+        scale_rows(1)
+        transposes(1)
+        regroup(1)
+        weight_regroup(1)
+        nc.vector.quantize_mx(
+            out=w_codes[:].rearrange("p c o -> p (c o)").bitcast(FP8X4),
+            scales=w_scl[:].rearrange("p c o -> p (c o)"),
+            in_=w_grp[:].rearrange("p c o t -> p (c o t)"),
+        )
+
+        bias_ps = psum_o.tile([P, OUTF], F32, name="bias_ps", tag="o")
+        nc.tensor.matmul(out=bias_ps[:], lhsT=ones_b[:], rhs=bias_row[:], start=True, stop=True)
+        bias_bc = const.tile([P, OUTF], F32, name="bias_bc")
+        nc.scalar.copy(out=bias_bc[:], in_=bias_ps[:])
+
+        for r in range(ROUNDS + 1):
+            nxt = r // 4 + 1
+            sums_now = r % 4 == 0 and nxt < GRAPHS
+            degrees_now = r % 4 == 1 and nxt < GRAPHS
+            if degrees_now:
+                degree_v(nxt)
+                degree_pe(nxt)
+                degree_sqrt(nxt)
+            if r + 2 < ROUNDS:
+                scale_rows(r + 2)
+                if r + 2 == 3:
+                    load_x(3, 0, 4)
+                    load_x(3, 4, 8)
+                transposes(r + 2)
+            if r < ROUNDS:
+                quantise(r)
+                if degrees_now:
+                    degree_recip(nxt)
+                products(r)
+            if sums_now:
+                col_sums(nxt)
+            if r + 2 < ROUNDS:
+                regroup(r + 2)
+            if r >= 1:
+                epilogue(r - 1)

@@ -53,7 +53,6 @@ def tile_gcn_t_kernel(tc, x, mask, weight, bias, out):
         nc.vector.memset(one_col[:], 1.0)
         bias_row = const.tile([P, OUTF], BF16, name="bias_row")
         nc.vector.memset(bias_row[:], 0.0)
-        nc.scalar.dma_start(out=bias_row[0:1, :], in_=bv)
         warm = const.tile([P, 1], F32, name="warm")
         nc.scalar.sqrt(out=warm[:], in_=one_col[:])
         ones_b = const.tile([P, P], BF16, name="ones_b")
@@ -79,14 +78,11 @@ def tile_gcn_t_kernel(tc, x, mask, weight, bias, out):
         cds = {}
         ops = {}
 
-        def load_mask(g):
-            m = mpool.tile([P, MC, MT, NODES], BF16, name="m%d" % g, tag="m")
-            mtiles[g] = m
-            if g == 0:
-                for c in range(MC):
-                    nc.sync.dma_start(out=m[:, c], in_=mg[g][:, c])
-            else:
-                nc.sync.dma_start(out=m[:], in_=mg[g])
+        def load_mask(g, c0, c1):
+            if g not in mtiles:
+                mtiles[g] = mpool.tile([P, MC, MT, NODES], BF16, name="m%d" % g, tag="m")
+            for c in range(c0, c1):
+                nc.sync.dma_start(out=mtiles[g][:, c], in_=mg[g][:, c])
 
         def self_loops(g):
             m = mtiles[g]
@@ -109,20 +105,21 @@ def tile_gcn_t_kernel(tc, x, mask, weight, bias, out):
                 xs[g] = xpool.tile([P, XT, FEAT], BF16, name="x%d" % g, tag="x")
             nc.sync.dma_start(out=xs[g][:, t0:t1, :], in_=xg[g][:, t0:t1, :])
 
-        def col_sums(g):
+        def col_sums(g, c):
             m = mtiles[g]
-            d_ps = psum_d.tile([P, MC, 8, NK], F32, name="d_ps%d" % g, tag="d")
-            dps[g] = d_ps
-            for c in range(MC):
-                for ib in range(8):
-                    for t in range(MT):
-                        nc.tensor.matmul(
-                            out=d_ps[:, c, ib, :],
-                            lhsT=m[:, c, t, ib * P : (ib + 1) * P],
-                            rhs=ones_b[:, 0:NK],
-                            start=(t == 0),
-                            stop=(t == MT - 1),
-                        )
+            if c == 0:
+                dps[g] = psum_d.tile([P, MC, 8, NK], F32, name="d_ps%d" % g, tag="d")
+            d_ps = dps[g]
+            blocks = [ib for ib in range(8) if ib // 2 != c] + [2 * c, 2 * c + 1]
+            for ib in blocks:
+                for t in range(MT):
+                    nc.tensor.matmul(
+                        out=d_ps[:, c, ib, :],
+                        lhsT=m[:, c, t, ib * P : (ib + 1) * P],
+                        rhs=ones_b[:, 0:NK],
+                        start=(t == 0),
+                        stop=(t == MT - 1),
+                    )
 
         spread = {}
 
@@ -185,13 +182,14 @@ def tile_gcn_t_kernel(tc, x, mask, weight, bias, out):
                 for kb in range(8):
                     nc.tensor.transpose(xt[:, kb, :], hs[r][:, s, kb * P : (kb + 1) * P], ident_b[:])
 
-        def regroup(r):
-            grp = gpool.tile([P, 2, 2, P, 4], BF16, name="grp%d" % r, tag="grp", align_bytes=64)
-            grps[r] = grp
-            for s in range(2):
-                nc.scalar.copy(
-                    out=grp[:, s], in_=xts[(r, s)][:].rearrange("p (c t) i -> p c i t", c=2)
+        def regroup(r, s):
+            if s == 0:
+                grps[r] = gpool.tile(
+                    [P, 2, 2, P, 4], BF16, name="grp%d" % r, tag="grp", align_bytes=64
                 )
+            nc.scalar.copy(
+                out=grps[r][:, s], in_=xts[(r, s)][:].rearrange("p (c t) i -> p c i t", c=2)
+            )
 
         def quantise(r):
             codes = cpool.tile([P, 4 * P], U32, name="codes%d" % r, tag="codes", align_bytes=64)
@@ -228,31 +226,47 @@ def tile_gcn_t_kernel(tc, x, mask, weight, bias, out):
                     out=o_sb[:, s, :], in0=ops[(r, s)][:], in1=bias_bc[:], op=ALU.add
                 )
             nc.scalar.activation(out=o_sb[:, 0, :], in_=o_sb[:, 0, :], func=ACT.Relu)
+            if r == ROUNDS - 1:
+                nc.sync.dma_start(out=og[g][:, 2 * q, :], in_=o_sb[:, 0, :])
             nc.vector.tensor_scalar_max(out=o_sb[:, 1, :], in0=o_sb[:, 1, :], scalar1=0.0)
-            nc.sync.dma_start(out=og[g][:, 2 * q : 2 * q + 2, :], in_=o_sb[:])
+            if r == ROUNDS - 1:
+                nc.sync.dma_start(out=og[g][:, 2 * q + 1, :], in_=o_sb[:, 1, :])
+            else:
+                nc.sync.dma_start(out=og[g][:, 2 * q : 2 * q + 2, :], in_=o_sb[:])
 
-        load_mask(0)
-        load_x(0, 0, 2)
+        load_mask(0, 0, 2)
+        nc.sync.dma_start(out=bias_row[0:1, :], in_=bv)
+        load_mask(0, 2, 4)
         w_raw = const.tile([P, 2, 4, OUTF], BF16, name="w_raw")
         nc.sync.dma_start(out=w_raw[:], in_=wv)
+        load_x(0, 0, 2)
         load_x(0, 2, 4)
-        load_x(0, 4, 8)
-        load_mask(1)
+        load_mask(1, 0, 2)
+        load_x(0, 4, 6)
+        load_mask(1, 2, 4)
+        load_x(0, 6, 8)
         load_x(1, 0, 4)
+        load_mask(2, 0, 2)
         load_x(1, 4, 8)
-        load_mask(2)
+        load_mask(2, 2, 4)
         load_x(2, 0, 4)
         load_x(2, 4, 8)
         for g in range(3):
             self_loops(g)
 
-        col_sums(0)
-        load_mask(3)
+        col_sums(0, 0)
+        col_sums(0, 1)
+        bias_ps = psum_o.tile([P, OUTF], F32, name="bias_ps", tag="o")
+        nc.tensor.matmul(out=bias_ps[:], lhsT=ones_b[:], rhs=bias_row[:], start=True, stop=True)
+        bias_bc = const.tile([P, OUTF], F32, name="bias_bc")
+        nc.scalar.copy(out=bias_bc[:], in_=bias_ps[:])
+        col_sums(0, 2)
+        col_sums(0, 3)
+        load_mask(3, 0, 4)
         self_loops(3)
         degree_v(0)
         degree_pe(0)
         degree_sqrt(0)
-        degree_recip(0)
 
         w_grp = const.tile([P, 2, OUTF, 4], BF16, name="w_grp", align_bytes=64)
         w_codes = const.tile([P, 2, OUTF], U32, name="w_codes", align_bytes=64)
@@ -264,47 +278,52 @@ def tile_gcn_t_kernel(tc, x, mask, weight, bias, out):
                 in_=w_raw[:, c].rearrange("p t (a i) -> p a t i", i=4),
             )
 
+        weight_regroup(0)
+        degree_recip(0)
         scale_rows(0)
         transposes(0)
-        regroup(0)
-        weight_regroup(0)
+        regroup(0, 0)
+        regroup(0, 1)
+        weight_regroup(1)
         scale_rows(1)
         transposes(1)
-        regroup(1)
-        weight_regroup(1)
+        regroup(1, 0)
+        regroup(1, 1)
         nc.vector.quantize_mx(
             out=w_codes[:].rearrange("p c o -> p (c o)").bitcast(FP8X4),
             scales=w_scl[:].rearrange("p c o -> p (c o)"),
             in_=w_grp[:].rearrange("p c o t -> p (c o t)"),
         )
-
-        bias_ps = psum_o.tile([P, OUTF], F32, name="bias_ps", tag="o")
-        nc.tensor.matmul(out=bias_ps[:], lhsT=ones_b[:], rhs=bias_row[:], start=True, stop=True)
-        bias_bc = const.tile([P, OUTF], F32, name="bias_bc")
-        nc.scalar.copy(out=bias_bc[:], in_=bias_ps[:])
+        col_sums(1, 0)
+        col_sums(1, 1)
 
         for r in range(ROUNDS + 1):
             nxt = r // 4 + 1
-            sums_now = r % 4 == 0 and nxt < GRAPHS
             degrees_now = r % 4 == 1 and nxt < GRAPHS
-            if degrees_now:
-                degree_v(nxt)
-                degree_pe(nxt)
-                degree_sqrt(nxt)
+            sum_g, sum_c = divmod(r + 2, 4)
+            sum_g = sum_g + 1
             if r + 2 < ROUNDS:
                 scale_rows(r + 2)
                 if r + 2 == 3:
                     load_x(3, 0, 4)
                     load_x(3, 4, 8)
+            if sum_g < GRAPHS:
+                col_sums(sum_g, sum_c)
+            if r + 2 < ROUNDS:
                 transposes(r + 2)
             if r < ROUNDS:
                 quantise(r)
                 if degrees_now:
-                    degree_recip(nxt)
+                    degree_v(nxt)
                 products(r)
-            if sums_now:
-                col_sums(nxt)
+                if degrees_now:
+                    degree_pe(nxt)
             if r + 2 < ROUNDS:
-                regroup(r + 2)
+                regroup(r + 2, 0)
+                if degrees_now:
+                    degree_sqrt(nxt)
+                regroup(r + 2, 1)
             if r >= 1:
                 epilogue(r - 1)
+            if degrees_now:
+                degree_recip(nxt)

@@ -22,6 +22,19 @@ MC = 4
 MT = 2
 NK = 16
 ROUNDS = 16
+WARM = 2
+SUMS_AT = {
+    (0, 0): [(1, 2)],
+    (0, 1): [(1, 3)],
+    (2, 0): [(2, 0)],
+    (2, 1): [(2, 1)],
+    (3, 1): [(2, 2)],
+    (4, 0): [(2, 3)],
+    (6, 0): [(3, 0)],
+    (6, 1): [(3, 1)],
+    (7, 0): [(3, 2)],
+    (7, 1): [(3, 3)],
+}
 FLOPS = 2 * GRAPHS * NODES * FEAT * OUTF
 
 
@@ -175,12 +188,11 @@ def tile_gcn_t_kernel(tc, x, mask, weight, bias, out):
                     op0=ALU.mult,
                 )
 
-        def transposes(r):
-            for s in range(2):
-                xt = psum_t.tile([P, 8, P], BF16, name="xt%d_%d" % (r, s), tag="xt")
-                xts[(r, s)] = xt
-                for kb in range(8):
-                    nc.tensor.transpose(xt[:, kb, :], hs[r][:, s, kb * P : (kb + 1) * P], ident_b[:])
+        def transposes(r, s):
+            xt = psum_t.tile([P, 8, P], BF16, name="xt%d_%d" % (r, s), tag="xt")
+            xts[(r, s)] = xt
+            for kb in range(8):
+                nc.tensor.transpose(xt[:, kb, :], hs[r][:, s, kb * P : (kb + 1) * P], ident_b[:])
 
         def regroup(r, s):
             if s == 0:
@@ -201,33 +213,42 @@ def tile_gcn_t_kernel(tc, x, mask, weight, bias, out):
                 in_=grps[r][:].rearrange("p s c i t -> p (s c i t)"),
             )
 
-        def products(r):
+        def products(r, s):
             codes, scl = cds[r]
-            for s in range(2):
-                o_ps = psum_o.tile([P, OUTF], F32, name="o_ps%d_%d" % (r, s), tag="o")
-                ops[(r, s)] = o_ps
-                for c in range(2):
-                    cols = slice((2 * s + c) * P, (2 * s + c + 1) * P)
-                    nc.tensor.matmul_mx(
-                        out=o_ps[:],
-                        lhsT=codes[:, cols].bitcast(FP8X4),
-                        lhsT_scale=scl[:, cols],
-                        rhs=w_codes[:, c, :].bitcast(FP8X4),
-                        rhs_scale=w_scl[:, c, :],
-                        start=(c == 0),
-                        stop=(c == 1),
-                    )
+            o_ps = psum_o.tile([P, OUTF], F32, name="o_ps%d_%d" % (r, s), tag="o")
+            ops[(r, s)] = o_ps
+            for c in range(2):
+                cols = slice((2 * s + c) * P, (2 * s + c + 1) * P)
+                nc.tensor.matmul_mx(
+                    out=o_ps[:],
+                    lhsT=codes[:, cols].bitcast(FP8X4),
+                    lhsT_scale=scl[:, cols],
+                    rhs=w_codes[:, c, :].bitcast(FP8X4),
+                    rhs_scale=w_scl[:, c, :],
+                    start=(c == 0),
+                    stop=(c == 1),
+                )
 
-        def epilogue(r):
-            g, q = divmod(r, 4)
+        osbs = {}
+
+        def add_bias(r):
             o_sb = opool.tile([P, 2, OUTF], F32, name="o_sb%d" % r, tag="o_sb")
+            osbs[r] = o_sb
             for s in range(2):
                 nc.vector.tensor_tensor(
                     out=o_sb[:, s, :], in0=ops[(r, s)][:], in1=bias_bc[:], op=ALU.add
                 )
+
+        def relu_scalar(r):
+            g, q = divmod(r, 4)
+            o_sb = osbs[r]
             nc.scalar.activation(out=o_sb[:, 0, :], in_=o_sb[:, 0, :], func=ACT.Relu)
             if r == ROUNDS - 1:
                 nc.sync.dma_start(out=og[g][:, 2 * q, :], in_=o_sb[:, 0, :])
+
+        def relu_vector_store(r):
+            g, q = divmod(r, 4)
+            o_sb = osbs[r]
             nc.vector.tensor_scalar_max(out=o_sb[:, 1, :], in0=o_sb[:, 1, :], scalar1=0.0)
             if r == ROUNDS - 1:
                 nc.sync.dma_start(out=og[g][:, 2 * q + 1, :], in_=o_sb[:, 1, :])
@@ -245,7 +266,8 @@ def tile_gcn_t_kernel(tc, x, mask, weight, bias, out):
         load_x(0, 4, 6)
         load_mask(1, 2, 4)
         load_x(0, 6, 8)
-        load_x(1, 0, 4)
+        load_x(1, 0, 2)
+        load_x(1, 2, 4)
         load_mask(2, 0, 2)
         load_x(1, 4, 8)
         load_mask(2, 2, 4)
@@ -254,18 +276,27 @@ def tile_gcn_t_kernel(tc, x, mask, weight, bias, out):
         for g in range(3):
             self_loops(g)
 
+        bias_ps = psum_o.tile([P, OUTF], F32, name="bias_ps", tag="o")
+
+        def bias_matmul(times):
+            for i in range(times):
+                nc.tensor.matmul(
+                    out=bias_ps[:], lhsT=ones_b[:], rhs=bias_row[:], start=True, stop=True
+                )
+
         col_sums(0, 0)
         col_sums(0, 1)
-        bias_ps = psum_o.tile([P, OUTF], F32, name="bias_ps", tag="o")
-        nc.tensor.matmul(out=bias_ps[:], lhsT=ones_b[:], rhs=bias_row[:], start=True, stop=True)
+        bias_matmul(1)
         bias_bc = const.tile([P, OUTF], F32, name="bias_bc")
         nc.scalar.copy(out=bias_bc[:], in_=bias_ps[:])
         col_sums(0, 2)
         col_sums(0, 3)
+        bias_matmul(WARM)
         load_mask(3, 0, 4)
         self_loops(3)
         degree_v(0)
         degree_pe(0)
+        bias_matmul(WARM)
         degree_sqrt(0)
 
         w_grp = const.tile([P, 2, OUTF, 4], BF16, name="w_grp", align_bytes=64)
@@ -280,15 +311,15 @@ def tile_gcn_t_kernel(tc, x, mask, weight, bias, out):
 
         weight_regroup(0)
         degree_recip(0)
-        scale_rows(0)
-        transposes(0)
-        regroup(0, 0)
-        regroup(0, 1)
-        weight_regroup(1)
-        scale_rows(1)
-        transposes(1)
-        regroup(1, 0)
-        regroup(1, 1)
+        for r in range(2):
+            scale_rows(r)
+            transposes(r, 0)
+            bias_matmul(WARM)
+            transposes(r, 1)
+            regroup(r, 0)
+            regroup(r, 1)
+            if r == 0:
+                weight_regroup(1)
         nc.vector.quantize_mx(
             out=w_codes[:].rearrange("p c o -> p (c o)").bitcast(FP8X4),
             scales=w_scl[:].rearrange("p c o -> p (c o)"),
@@ -296,34 +327,40 @@ def tile_gcn_t_kernel(tc, x, mask, weight, bias, out):
         )
         col_sums(1, 0)
         col_sums(1, 1)
+        bias_matmul(WARM)
 
         for r in range(ROUNDS + 1):
             nxt = r // 4 + 1
             degrees_now = r % 4 == 1 and nxt < GRAPHS
-            sum_g, sum_c = divmod(r + 2, 4)
-            sum_g = sum_g + 1
             if r + 2 < ROUNDS:
                 scale_rows(r + 2)
                 if r + 2 == 3:
                     load_x(3, 0, 4)
                     load_x(3, 4, 8)
-            if sum_g < GRAPHS:
-                col_sums(sum_g, sum_c)
-            if r + 2 < ROUNDS:
-                transposes(r + 2)
             if r < ROUNDS:
                 quantise(r)
-                if degrees_now:
-                    degree_v(nxt)
-                products(r)
-                if degrees_now:
+            if degrees_now:
+                degree_v(nxt)
+            for s in range(2):
+                if r + 2 < ROUNDS:
+                    transposes(r + 2, s)
+                if r < ROUNDS:
+                    products(r, s)
+                for g, c in SUMS_AT.get((r, s), []):
+                    col_sums(g, c)
+                if degrees_now and s == 0:
                     degree_pe(nxt)
+            if r >= 1:
+                add_bias(r - 1)
             if r + 2 < ROUNDS:
                 regroup(r + 2, 0)
-                if degrees_now:
-                    degree_sqrt(nxt)
+            if degrees_now:
+                degree_sqrt(nxt)
+            if r >= 1:
+                relu_scalar(r - 1)
+            if r + 2 < ROUNDS:
                 regroup(r + 2, 1)
             if r >= 1:
-                epilogue(r - 1)
+                relu_vector_store(r - 1)
             if degrees_now:
                 degree_recip(nxt)

@@ -97,10 +97,10 @@ def tile_gcn_t_kernel(tc, x, mask, weight, bias, out):
             for c in range(c0, c1):
                 nc.sync.dma_start(out=mtiles[g][:, c], in_=mg[g][:, c])
 
-        def self_loops(g):
+        def self_loops(g, chunks):
             m = mtiles[g]
             w = P * MT
-            for c in range(MC):
+            for c in chunks:
                 for t in range(MT):
                     region = m[:, c, t, c * w : (c + 1) * w]
                     nc.gpsimd.affine_select(
@@ -239,12 +239,21 @@ def tile_gcn_t_kernel(tc, x, mask, weight, bias, out):
                     out=o_sb[:, s, :], in0=ops[(r, s)][:], in1=bias_bc[:], op=ALU.add
                 )
 
-        def relu_scalar(r):
+        def relu_first(r):
             g, q = divmod(r, 4)
             o_sb = osbs[r]
-            nc.scalar.activation(out=o_sb[:, 0, :], in_=o_sb[:, 0, :], func=ACT.Relu)
             if r == ROUNDS - 1:
+                nc.scalar.activation(out=o_sb[:, 0, :], in_=o_sb[:, 0, :], func=ACT.Relu)
                 nc.sync.dma_start(out=og[g][:, 2 * q, :], in_=o_sb[:, 0, :])
+            else:
+                nc.gpsimd.tensor_scalar(
+                    out=o_sb[:, 0, :],
+                    in0=o_sb[:, 0, :],
+                    scalar1=float("inf"),
+                    scalar2=0.0,
+                    op0=ALU.min,
+                    op1=ALU.max,
+                )
 
         def relu_vector_store(r):
             g, q = divmod(r, 4)
@@ -273,8 +282,8 @@ def tile_gcn_t_kernel(tc, x, mask, weight, bias, out):
         load_mask(2, 2, 4)
         load_x(2, 0, 4)
         load_x(2, 4, 8)
-        for g in range(3):
-            self_loops(g)
+        for g in range(2):
+            self_loops(g, range(MC))
 
         bias_ps = psum_o.tile([P, OUTF], F32, name="bias_ps", tag="o")
 
@@ -293,7 +302,6 @@ def tile_gcn_t_kernel(tc, x, mask, weight, bias, out):
         col_sums(0, 3)
         bias_matmul(WARM)
         load_mask(3, 0, 4)
-        self_loops(3)
         degree_v(0)
         degree_pe(0)
         bias_matmul(WARM)
@@ -332,6 +340,9 @@ def tile_gcn_t_kernel(tc, x, mask, weight, bias, out):
         for r in range(ROUNDS + 1):
             nxt = r // 4 + 1
             degrees_now = r % 4 == 1 and nxt < GRAPHS
+            for s in range(2):
+                for g, c in SUMS_AT.get((r + 1, s), []):
+                    self_loops(g, [c])
             if r + 2 < ROUNDS:
                 scale_rows(r + 2)
                 if r + 2 == 3:
@@ -357,7 +368,7 @@ def tile_gcn_t_kernel(tc, x, mask, weight, bias, out):
             if degrees_now:
                 degree_sqrt(nxt)
             if r >= 1:
-                relu_scalar(r - 1)
+                relu_first(r - 1)
             if r + 2 < ROUNDS:
                 regroup(r + 2, 1)
             if r >= 1:

@@ -97,10 +97,10 @@ def tile_gcn_t_kernel(tc, x, mask, weight, bias, out):
             for c in range(c0, c1):
                 nc.sync.dma_start(out=mtiles[g][:, c], in_=mg[g][:, c])
 
-        def self_loops(g, chunks):
+        def self_loops(g):
             m = mtiles[g]
             w = P * MT
-            for c in chunks:
+            for c in range(MC):
                 for t in range(MT):
                     region = m[:, c, t, c * w : (c + 1) * w]
                     nc.gpsimd.affine_select(
@@ -207,11 +207,20 @@ def tile_gcn_t_kernel(tc, x, mask, weight, bias, out):
             codes = cpool.tile([P, 4 * P], U32, name="codes%d" % r, tag="codes", align_bytes=64)
             scl = cpool.tile([P, 4 * P], U8, name="scl%d" % r, tag="scl", align_bytes=64)
             cds[r] = (codes, scl)
-            nc.vector.quantize_mx(
-                out=codes[:].bitcast(FP8X4),
-                scales=scl[:],
-                in_=grps[r][:].rearrange("p s c i t -> p (s c i t)"),
-            )
+            if r == ROUNDS - 1:
+                for s in range(2):
+                    cols = slice(2 * s * P, 2 * (s + 1) * P)
+                    nc.vector.quantize_mx(
+                        out=codes[:, cols].bitcast(FP8X4),
+                        scales=scl[:, cols],
+                        in_=grps[r][:, s].rearrange("p c i t -> p (c i t)"),
+                    )
+            else:
+                nc.vector.quantize_mx(
+                    out=codes[:].bitcast(FP8X4),
+                    scales=scl[:],
+                    in_=grps[r][:].rearrange("p s c i t -> p (s c i t)"),
+                )
 
         def products(r, s):
             codes, scl = cds[r]
@@ -239,26 +248,20 @@ def tile_gcn_t_kernel(tc, x, mask, weight, bias, out):
                     out=o_sb[:, s, :], in0=ops[(r, s)][:], in1=bias_bc[:], op=ALU.add
                 )
 
-        def relu_first(r):
+        def relu_scalar(r):
             g, q = divmod(r, 4)
             o_sb = osbs[r]
+            nc.scalar.activation(out=o_sb[:, 0, :], in_=o_sb[:, 0, :], func=ACT.Relu)
             if r == ROUNDS - 1:
-                nc.scalar.activation(out=o_sb[:, 0, :], in_=o_sb[:, 0, :], func=ACT.Relu)
                 nc.sync.dma_start(out=og[g][:, 2 * q, :], in_=o_sb[:, 0, :])
-            else:
-                nc.gpsimd.tensor_scalar(
-                    out=o_sb[:, 0, :],
-                    in0=o_sb[:, 0, :],
-                    scalar1=float("inf"),
-                    scalar2=0.0,
-                    op0=ALU.min,
-                    op1=ALU.max,
-                )
 
         def relu_vector_store(r):
             g, q = divmod(r, 4)
             o_sb = osbs[r]
-            nc.vector.tensor_scalar_max(out=o_sb[:, 1, :], in0=o_sb[:, 1, :], scalar1=0.0)
+            if r in (ROUNDS - 3, ROUNDS - 2):
+                nc.scalar.activation(out=o_sb[:, 1, :], in_=o_sb[:, 1, :], func=ACT.Relu)
+            else:
+                nc.vector.tensor_scalar_max(out=o_sb[:, 1, :], in0=o_sb[:, 1, :], scalar1=0.0)
             if r == ROUNDS - 1:
                 nc.sync.dma_start(out=og[g][:, 2 * q + 1, :], in_=o_sb[:, 1, :])
             else:
@@ -282,8 +285,8 @@ def tile_gcn_t_kernel(tc, x, mask, weight, bias, out):
         load_mask(2, 2, 4)
         load_x(2, 0, 4)
         load_x(2, 4, 8)
-        for g in range(2):
-            self_loops(g, range(MC))
+        for g in range(3):
+            self_loops(g)
 
         bias_ps = psum_o.tile([P, OUTF], F32, name="bias_ps", tag="o")
 
@@ -302,6 +305,7 @@ def tile_gcn_t_kernel(tc, x, mask, weight, bias, out):
         col_sums(0, 3)
         bias_matmul(WARM)
         load_mask(3, 0, 4)
+        self_loops(3)
         degree_v(0)
         degree_pe(0)
         bias_matmul(WARM)
@@ -340,9 +344,6 @@ def tile_gcn_t_kernel(tc, x, mask, weight, bias, out):
         for r in range(ROUNDS + 1):
             nxt = r // 4 + 1
             degrees_now = r % 4 == 1 and nxt < GRAPHS
-            for s in range(2):
-                for g, c in SUMS_AT.get((r + 1, s), []):
-                    self_loops(g, [c])
             if r + 2 < ROUNDS:
                 scale_rows(r + 2)
                 if r + 2 == 3:
@@ -352,25 +353,29 @@ def tile_gcn_t_kernel(tc, x, mask, weight, bias, out):
                 quantise(r)
             if degrees_now:
                 degree_v(nxt)
+            if r + 2 < ROUNDS:
+                transposes(r + 2, 0)
+                transposes(r + 2, 1)
+            if r < ROUNDS:
+                products(r, 0)
+                products(r, 1)
             for s in range(2):
-                if r + 2 < ROUNDS:
-                    transposes(r + 2, s)
-                if r < ROUNDS:
-                    products(r, s)
                 for g, c in SUMS_AT.get((r, s), []):
                     col_sums(g, c)
-                if degrees_now and s == 0:
-                    degree_pe(nxt)
+            if degrees_now:
+                degree_pe(nxt)
             if r >= 1:
                 add_bias(r - 1)
             if r + 2 < ROUNDS:
                 regroup(r + 2, 0)
             if degrees_now:
                 degree_sqrt(nxt)
-            if r >= 1:
-                relu_first(r - 1)
+            if r >= 1 and r + 2 != ROUNDS - 1:
+                relu_scalar(r - 1)
             if r + 2 < ROUNDS:
                 regroup(r + 2, 1)
+            if r >= 1 and r + 2 == ROUNDS - 1:
+                relu_scalar(r - 1)
             if r >= 1:
                 relu_vector_store(r - 1)
             if degrees_now:

@@ -13,52 +13,61 @@ ACT = mybir.ActivationFunctionType
 AX = mybir.AxisListType
 
 P = 128
+PACK = 4
 GRAPHS = 4
 NODES = 1024
 FEAT = 1024
 OUTF = 512
-XT = 8
-MC = 4
-MT = 2
-NK = 16
-ROUNDS = 16
-WARM = 2
-SUMS_AT = {
-    (0, 0): [(1, 2)],
-    (0, 1): [(1, 3)],
-    (2, 0): [(2, 0)],
-    (2, 1): [(2, 1)],
-    (3, 1): [(2, 2)],
-    (4, 0): [(2, 3)],
-    (6, 0): [(3, 0)],
-    (6, 1): [(3, 1)],
-    (7, 0): [(3, 2)],
-    (7, 1): [(3, 3)],
-}
+PASSES = FEAT // (P * PACK)
+BLOCKS = FEAT // P
+SLICES = NODES // P
+PAIR = 2
+ROUNDS_PER_GRAPH = SLICES // PAIR
+ROUNDS = GRAPHS * ROUNDS_PER_GRAPH
+LEAD = 2
+CHUNKS = 4
+CHUNK_ROWS = 2
+SUM_COLS = 16
+SPREAD = P // SLICES
+CLOCK_REPEATS = 2
+RESIDENT = 3
+RESULT_BUFS = 12
+LOOP = 1.0
 FLOPS = 2 * GRAPHS * NODES * FEAT * OUTF
 
 
 def tile_gcn_t_kernel(tc, x, mask, weight, bias, out):
     nc = tc.nc
-    xg = x.rearrange("a b (p t) k -> (a b) p t k", t=XT)
-    mg = mask.rearrange("a b (c p t) i -> (a b) p c t i", c=MC, p=P, t=MT)
-    og = out.rearrange("a b (p t) o -> (a b) p t o", t=XT)
-    wv = weight.rearrange("(c t p) o -> p c t o", c=2, t=4, p=P)
-    bv = bias.rearrange("(r n) -> r n", r=1)
+    x_view = x.rearrange("a b (p t) k -> (a b) p t k", t=SLICES)
+    out_view = out.rearrange("a b (p t) o -> (a b) p t o", t=SLICES)
+    mask_view = mask.rearrange("a b (c p t) i -> (a b) p c t i", c=CHUNKS, p=P, t=CHUNK_ROWS)
+    weight_view = weight.rearrange("(c t p) o -> p c t o", c=PASSES, t=PACK, p=P)
+    bias_view = bias.rearrange("(r n) -> r n", r=1)
 
     with ExitStack() as ctx:
         const = ctx.enter_context(tc.tile_pool(name="const", bufs=1))
-        mpool = ctx.enter_context(tc.tile_pool(name="mpool", bufs=3))
-        xpool = ctx.enter_context(tc.tile_pool(name="xpool", bufs=3))
-        hpool = ctx.enter_context(tc.tile_pool(name="hpool", bufs=3))
-        gpool = ctx.enter_context(tc.tile_pool(name="gpool", bufs=3))
-        cpool = ctx.enter_context(tc.tile_pool(name="cpool", bufs=3))
+        mask_pool = ctx.enter_context(tc.tile_pool(name="mask_pool", bufs=RESIDENT))
+        x_pool = ctx.enter_context(tc.tile_pool(name="x_pool", bufs=RESIDENT))
+        work = ctx.enter_context(tc.tile_pool(name="work", bufs=LEAD + 1))
         small = ctx.enter_context(tc.tile_pool(name="small", bufs=2))
-        opool = ctx.enter_context(tc.tile_pool(name="opool", bufs=12))
+        result_pool = ctx.enter_context(tc.tile_pool(name="result_pool", bufs=RESULT_BUFS))
         psum_t = ctx.enter_context(tc.psum_pool(name="psum_t", bufs=3))
         psum_o = ctx.enter_context(tc.psum_pool(name="psum_o", bufs=4))
         psum_d = ctx.enter_context(tc.psum_pool(name="psum_d", bufs=1))
         ctx.enter_context(tc.manual_schedule())
+
+        mask_tiles = {}
+        x_tiles = {}
+        sum_banks = {}
+        spread_tiles = {}
+        root_tiles = {}
+        inv_sqrt_d = {}
+        scaled = {}
+        flipped = {}
+        grouped = {}
+        packed = {}
+        products = {}
+        results = {}
 
         ident_f = const.tile([P, P], F32, name="ident_f")
         make_identity(nc, ident_f[:])
@@ -66,212 +75,213 @@ def tile_gcn_t_kernel(tc, x, mask, weight, bias, out):
         nc.vector.memset(one_col[:], 1.0)
         bias_row = const.tile([P, OUTF], BF16, name="bias_row")
         nc.vector.memset(bias_row[:], 0.0)
-        warm = const.tile([P, 1], F32, name="warm")
-        nc.scalar.sqrt(out=warm[:], in_=one_col[:])
+        first_sqrt = const.tile([P, 1], F32, name="first_sqrt")
+        nc.scalar.sqrt(out=first_sqrt[:], in_=one_col[:])
         ones_b = const.tile([P, P], BF16, name="ones_b")
         nc.vector.memset(ones_b[:], 1.0)
         ident_b = const.tile([P, P], BF16, name="ident_b")
         nc.vector.tensor_copy(out=ident_b[:], in_=ident_f[:])
-        e_sel = const.tile([P, 8], F32, name="e_sel")
+        row_in_group = const.tile([P, SLICES], F32, name="row_in_group")
         nc.vector.tensor_reduce(
-            out=e_sel[:], in_=ident_f[:].rearrange("p (q t) -> p t q", t=8), axis=AX.X, op=ALU.add
+            out=row_in_group[:],
+            in_=ident_f[:].rearrange("p (q t) -> p t q", t=SLICES),
+            axis=AX.X,
+            op=ALU.add,
         )
-        g_sel = const.tile([P, 16], F32, name="g_sel")
+        group_of_row = const.tile([P, SPREAD], F32, name="group_of_row")
         nc.vector.tensor_reduce(
-            out=g_sel[:], in_=ident_f[:].rearrange("p (q t) -> p q t", t=8), axis=AX.X, op=ALU.add
+            out=group_of_row[:],
+            in_=ident_f[:].rearrange("p (q t) -> p q t", t=SLICES),
+            axis=AX.X,
+            op=ALU.add,
         )
+        bias_all = const.tile([P, OUTF], F32, name="bias_all")
+        w_raw = const.tile([P, PASSES, PACK, OUTF], BF16, name="w_raw")
+        w_grouped = const.tile([P, PASSES, OUTF, PACK], BF16, name="w_grouped", align_bytes=64)
+        w_words = const.tile([P, PASSES, OUTF], U32, name="w_words", align_bytes=64)
+        w_scales = const.tile([P, PASSES, OUTF], U8, name="w_scales", align_bytes=64)
+        bias_bank = psum_o.tile([P, OUTF], F32, name="bias_bank", tag="o")
 
-        mtiles = {}
-        xs = {}
-        rss = {}
-        dps = {}
-        hs = {}
-        xts = {}
-        grps = {}
-        cds = {}
-        ops = {}
+        def load_mask(g, first_chunk, end_chunk):
+            if g not in mask_tiles:
+                mask_tiles[g] = mask_pool.tile(
+                    [P, CHUNKS, CHUNK_ROWS, NODES], BF16, name="mask%d" % g, tag="mask"
+                )
+            for c in range(first_chunk, end_chunk):
+                nc.sync.dma_start(out=mask_tiles[g][:, c], in_=mask_view[g][:, c])
 
-        def load_mask(g, c0, c1):
-            if g not in mtiles:
-                mtiles[g] = mpool.tile([P, MC, MT, NODES], BF16, name="m%d" % g, tag="m")
-            for c in range(c0, c1):
-                nc.sync.dma_start(out=mtiles[g][:, c], in_=mg[g][:, c])
+        def load_x(g, first_slice, end_slice):
+            if g not in x_tiles:
+                x_tiles[g] = x_pool.tile([P, SLICES, FEAT], BF16, name="x%d" % g, tag="x")
+            rows = slice(first_slice, end_slice)
+            nc.sync.dma_start(out=x_tiles[g][:, rows, :], in_=x_view[g][:, rows, :])
 
         def self_loops(g):
-            m = mtiles[g]
-            w = P * MT
-            for c in range(MC):
-                for t in range(MT):
-                    region = m[:, c, t, c * w : (c + 1) * w]
+            width = P * CHUNK_ROWS
+            for c in range(CHUNKS):
+                for t in range(CHUNK_ROWS):
+                    region = mask_tiles[g][:, c, t, c * width : (c + 1) * width]
                     nc.gpsimd.affine_select(
                         out=region,
                         in_=region,
-                        pattern=[[-1, w]],
+                        pattern=[[-1, width]],
                         compare_op=ALU.not_equal,
-                        fill=1.0,
+                        fill=LOOP,
                         base=t,
-                        channel_multiplier=MT,
+                        channel_multiplier=CHUNK_ROWS,
                     )
 
-        def load_x(g, t0, t1):
-            if g not in xs:
-                xs[g] = xpool.tile([P, XT, FEAT], BF16, name="x%d" % g, tag="x")
-            nc.sync.dma_start(out=xs[g][:, t0:t1, :], in_=xg[g][:, t0:t1, :])
-
-        def col_sums(g, c):
-            m = mtiles[g]
+        def column_sums(g, c):
             if c == 0:
-                dps[g] = psum_d.tile([P, MC, 8, NK], F32, name="d_ps%d" % g, tag="d")
-            d_ps = dps[g]
-            blocks = [ib for ib in range(8) if ib // 2 != c] + [2 * c, 2 * c + 1]
-            for ib in blocks:
-                for t in range(MT):
+                sum_banks[g] = psum_d.tile(
+                    [P, CHUNKS, BLOCKS, SUM_COLS], F32, name="sums%d" % g, tag="d"
+                )
+            with_diagonal = [CHUNK_ROWS * c + t for t in range(CHUNK_ROWS)]
+            for b in [b for b in range(BLOCKS) if b not in with_diagonal] + with_diagonal:
+                for t in range(CHUNK_ROWS):
                     nc.tensor.matmul(
-                        out=d_ps[:, c, ib, :],
-                        lhsT=m[:, c, t, ib * P : (ib + 1) * P],
-                        rhs=ones_b[:, 0:NK],
+                        out=sum_banks[g][:, c, b, :],
+                        lhsT=mask_tiles[g][:, c, t, b * P : (b + 1) * P],
+                        rhs=ones_b[:, 0:SUM_COLS],
                         start=(t == 0),
-                        stop=(t == MT - 1),
+                        stop=(t == CHUNK_ROWS - 1),
                     )
 
-        spread = {}
-
-        def degree_v(g):
-            d_sb = small.tile([P, 8], F32, name="d_sb%d" % g, tag="d_sb")
+        def degree_spread(g):
+            d_block = small.tile([P, BLOCKS], F32, name="d_block%d" % g, tag="d_block")
             nc.vector.tensor_reduce(
-                out=d_sb[:],
-                in_=dps[g][:].rearrange("p c i n -> p i c n")[:, :, :, 0],
+                out=d_block[:],
+                in_=sum_banks[g][:].rearrange("p c b n -> p b c n")[:, :, :, 0],
                 axis=AX.X,
                 op=ALU.add,
             )
-            w_t = small.tile([P, 8, 16], F32, name="spread%d" % g, tag="spread")
+            spread_tiles[g] = small.tile([P, BLOCKS, SPREAD], F32, name="spread%d" % g, tag="spread")
             nc.vector.tensor_tensor(
-                out=w_t[:],
-                in0=d_sb[:].unsqueeze(2).to_broadcast([P, 8, 16]),
-                in1=g_sel[:].unsqueeze(1).to_broadcast([P, 8, 16]),
+                out=spread_tiles[g][:],
+                in0=d_block[:].unsqueeze(2).to_broadcast([P, BLOCKS, SPREAD]),
+                in1=group_of_row[:].unsqueeze(1).to_broadcast([P, BLOCKS, SPREAD]),
                 op=ALU.mult,
             )
-            spread[g] = w_t
 
-        def degree_pe(g):
+        def degree_resort(g):
             nc.tensor.matmul(
-                out=dps[g][:, 0, 0, 0:8],
-                lhsT=spread[g][:].rearrange("p b q -> p (b q)"),
-                rhs=e_sel[:],
+                out=sum_banks[g][:, 0, 0, 0:SLICES],
+                lhsT=spread_tiles[g][:].rearrange("p b q -> p (b q)"),
+                rhs=row_in_group[:],
                 start=True,
                 stop=True,
             )
 
-        sqs = {}
+        def degree_root(g):
+            root_tiles[g] = small.tile([P, SLICES], F32, name="root%d" % g, tag="root")
+            nc.scalar.sqrt(out=root_tiles[g][:], in_=sum_banks[g][:, 0, 0, 0:SLICES])
 
-        def degree_sqrt(g):
-            sq = small.tile([P, 8], F32, name="sq%d" % g, tag="sq")
-            nc.scalar.sqrt(out=sq[:], in_=dps[g][:, 0, 0, 0:8])
-            sqs[g] = sq
+        def degree_reciprocal(g):
+            inv_sqrt_d[g] = small.tile([P, SLICES], F32, name="inv_sqrt_d%d" % g, tag="inv_sqrt_d")
+            nc.vector.reciprocal(out=inv_sqrt_d[g][:], in_=root_tiles[g][:])
 
-        def degree_recip(g):
-            rs = small.tile([P, 8], F32, name="rs%d" % g, tag="rs")
-            nc.vector.reciprocal(out=rs[:], in_=sqs[g][:])
-            rss[g] = rs
+        def bias_matmul(times):
+            for repeat in range(times):
+                nc.tensor.matmul(
+                    out=bias_bank[:], lhsT=ones_b[:], rhs=bias_row[:], start=True, stop=True
+                )
+
+        def weight_group(c):
+            nc.vector.tensor_copy(
+                out=w_grouped[:, c].rearrange("p (a i) t -> p a t i", i=4),
+                in_=w_raw[:, c].rearrange("p t (a i) -> p a t i", i=4),
+            )
 
         def scale_rows(r):
-            g, q = divmod(r, 4)
-            h = hpool.tile([P, 2, FEAT], BF16, name="h%d" % r, tag="h")
-            hs[r] = h
-            for s in range(2):
-                t = 2 * q + s
+            g, q = divmod(r, ROUNDS_PER_GRAPH)
+            scaled[r] = work.tile([P, PAIR, FEAT], BF16, name="scaled%d" % r, tag="scaled")
+            for s in range(PAIR):
+                t = PAIR * q + s
                 nc.vector.tensor_scalar(
-                    out=h[:, s, :],
-                    in0=xs[g][:, t, :],
-                    scalar1=rss[g][:, t : t + 1],
+                    out=scaled[r][:, s, :],
+                    in0=x_tiles[g][:, t, :],
+                    scalar1=inv_sqrt_d[g][:, t : t + 1],
                     scalar2=None,
                     op0=ALU.mult,
                 )
 
-        def transposes(r, s):
-            xt = psum_t.tile([P, 8, P], BF16, name="xt%d_%d" % (r, s), tag="xt")
-            xts[(r, s)] = xt
-            for kb in range(8):
-                nc.tensor.transpose(xt[:, kb, :], hs[r][:, s, kb * P : (kb + 1) * P], ident_b[:])
+        def transpose_slice(r, s):
+            bank = psum_t.tile([P, BLOCKS, P], BF16, name="flipped%d_%d" % (r, s), tag="t")
+            flipped[(r, s)] = bank
+            for b in range(BLOCKS):
+                nc.tensor.transpose(bank[:, b, :], scaled[r][:, s, b * P : (b + 1) * P], ident_b[:])
 
-        def regroup(r, s):
+        def group_slice(r, s):
             if s == 0:
-                grps[r] = gpool.tile(
-                    [P, 2, 2, P, 4], BF16, name="grp%d" % r, tag="grp", align_bytes=64
+                grouped[r] = work.tile(
+                    [P, PAIR, PASSES, P, PACK], BF16, name="grouped%d" % r, tag="grouped", align_bytes=64
                 )
             nc.scalar.copy(
-                out=grps[r][:, s], in_=xts[(r, s)][:].rearrange("p (c t) i -> p c i t", c=2)
+                out=grouped[r][:, s],
+                in_=flipped[(r, s)][:].rearrange("p (c t) i -> p c i t", c=PASSES),
             )
 
         def quantise(r):
-            codes = cpool.tile([P, 4 * P], U32, name="codes%d" % r, tag="codes", align_bytes=64)
-            scl = cpool.tile([P, 4 * P], U8, name="scl%d" % r, tag="scl", align_bytes=64)
-            cds[r] = (codes, scl)
+            width = PASSES * P
+            words = work.tile([P, PAIR * width], U32, name="words%d" % r, tag="words", align_bytes=64)
+            scales = work.tile([P, PAIR * width], U8, name="scales%d" % r, tag="scales", align_bytes=64)
+            packed[r] = (words, scales)
             if r == ROUNDS - 1:
-                for s in range(2):
-                    cols = slice(2 * s * P, 2 * (s + 1) * P)
+                for s in range(PAIR):
+                    cols = slice(s * width, (s + 1) * width)
                     nc.vector.quantize_mx(
-                        out=codes[:, cols].bitcast(FP8X4),
-                        scales=scl[:, cols],
-                        in_=grps[r][:, s].rearrange("p c i t -> p (c i t)"),
+                        out=words[:, cols].bitcast(FP8X4),
+                        scales=scales[:, cols],
+                        in_=grouped[r][:, s].rearrange("p c i t -> p (c i t)"),
                     )
             else:
                 nc.vector.quantize_mx(
-                    out=codes[:].bitcast(FP8X4),
-                    scales=scl[:],
-                    in_=grps[r][:].rearrange("p s c i t -> p (s c i t)"),
+                    out=words[:].bitcast(FP8X4),
+                    scales=scales[:],
+                    in_=grouped[r][:].rearrange("p s c i t -> p (s c i t)"),
                 )
 
-        def products(r, s):
-            codes, scl = cds[r]
-            o_ps = psum_o.tile([P, OUTF], F32, name="o_ps%d_%d" % (r, s), tag="o")
-            ops[(r, s)] = o_ps
-            for c in range(2):
-                cols = slice((2 * s + c) * P, (2 * s + c + 1) * P)
+        def multiply_slice(r, s):
+            words, scales = packed[r]
+            bank = psum_o.tile([P, OUTF], F32, name="product%d_%d" % (r, s), tag="o")
+            products[(r, s)] = bank
+            for c in range(PASSES):
+                cols = slice((PASSES * s + c) * P, (PASSES * s + c + 1) * P)
                 nc.tensor.matmul_mx(
-                    out=o_ps[:],
-                    lhsT=codes[:, cols].bitcast(FP8X4),
-                    lhsT_scale=scl[:, cols],
-                    rhs=w_codes[:, c, :].bitcast(FP8X4),
-                    rhs_scale=w_scl[:, c, :],
+                    out=bank[:],
+                    lhsT=words[:, cols].bitcast(FP8X4),
+                    lhsT_scale=scales[:, cols],
+                    rhs=w_words[:, c, :].bitcast(FP8X4),
+                    rhs_scale=w_scales[:, c, :],
                     start=(c == 0),
-                    stop=(c == 1),
+                    stop=(c == PASSES - 1),
                 )
-
-        osbs = {}
 
         def add_bias(r):
-            o_sb = opool.tile([P, 2, OUTF], F32, name="o_sb%d" % r, tag="o_sb")
-            osbs[r] = o_sb
-            for s in range(2):
+            results[r] = result_pool.tile([P, PAIR, OUTF], F32, name="result%d" % r, tag="result")
+            for s in range(PAIR):
                 nc.vector.tensor_tensor(
-                    out=o_sb[:, s, :], in0=ops[(r, s)][:], in1=bias_bc[:], op=ALU.add
+                    out=results[r][:, s, :], in0=products[(r, s)][:], in1=bias_all[:], op=ALU.add
                 )
 
-        def relu_scalar(r):
-            g, q = divmod(r, 4)
-            o_sb = osbs[r]
-            nc.scalar.activation(out=o_sb[:, 0, :], in_=o_sb[:, 0, :], func=ACT.Relu)
-            if r == ROUNDS - 1:
-                nc.sync.dma_start(out=og[g][:, 2 * q, :], in_=o_sb[:, 0, :])
+        def relu_slice(r, s, engine):
+            part = results[r][:, s, :]
+            if engine == "scalar":
+                nc.scalar.activation(out=part, in_=part, func=ACT.Relu)
+            else:
+                nc.vector.tensor_scalar_max(out=part, in0=part, scalar1=0.0)
 
-        def relu_vector_store(r):
-            g, q = divmod(r, 4)
-            o_sb = osbs[r]
-            if r in (ROUNDS - 3, ROUNDS - 2):
-                nc.scalar.activation(out=o_sb[:, 1, :], in_=o_sb[:, 1, :], func=ACT.Relu)
-            else:
-                nc.vector.tensor_scalar_max(out=o_sb[:, 1, :], in0=o_sb[:, 1, :], scalar1=0.0)
-            if r == ROUNDS - 1:
-                nc.sync.dma_start(out=og[g][:, 2 * q + 1, :], in_=o_sb[:, 1, :])
-            else:
-                nc.sync.dma_start(out=og[g][:, 2 * q : 2 * q + 2, :], in_=o_sb[:])
+        def store(r, first_slice, end_slice):
+            g, q = divmod(r, ROUNDS_PER_GRAPH)
+            nc.sync.dma_start(
+                out=out_view[g][:, PAIR * q + first_slice : PAIR * q + end_slice, :],
+                in_=results[r][:, first_slice:end_slice, :],
+            )
 
         load_mask(0, 0, 2)
-        nc.sync.dma_start(out=bias_row[0:1, :], in_=bv)
+        nc.sync.dma_start(out=bias_row[0:1, :], in_=bias_view)
         load_mask(0, 2, 4)
-        w_raw = const.tile([P, 2, 4, OUTF], BF16, name="w_raw")
-        nc.sync.dma_start(out=w_raw[:], in_=wv)
+        nc.sync.dma_start(out=w_raw[:], in_=weight_view)
         load_x(0, 0, 2)
         load_x(0, 2, 4)
         load_mask(1, 0, 2)
@@ -285,98 +295,93 @@ def tile_gcn_t_kernel(tc, x, mask, weight, bias, out):
         load_mask(2, 2, 4)
         load_x(2, 0, 4)
         load_x(2, 4, 8)
-        for g in range(3):
+        for g in range(RESIDENT):
             self_loops(g)
 
-        bias_ps = psum_o.tile([P, OUTF], F32, name="bias_ps", tag="o")
-
-        def bias_matmul(times):
-            for i in range(times):
-                nc.tensor.matmul(
-                    out=bias_ps[:], lhsT=ones_b[:], rhs=bias_row[:], start=True, stop=True
-                )
-
-        col_sums(0, 0)
-        col_sums(0, 1)
+        column_sums(0, 0)
+        column_sums(0, 1)
         bias_matmul(1)
-        bias_bc = const.tile([P, OUTF], F32, name="bias_bc")
-        nc.scalar.copy(out=bias_bc[:], in_=bias_ps[:])
-        col_sums(0, 2)
-        col_sums(0, 3)
-        bias_matmul(WARM)
+        nc.scalar.copy(out=bias_all[:], in_=bias_bank[:])
+        column_sums(0, 2)
+        column_sums(0, 3)
+        bias_matmul(CLOCK_REPEATS)
         load_mask(3, 0, 4)
         self_loops(3)
-        degree_v(0)
-        degree_pe(0)
-        bias_matmul(WARM)
-        degree_sqrt(0)
-
-        w_grp = const.tile([P, 2, OUTF, 4], BF16, name="w_grp", align_bytes=64)
-        w_codes = const.tile([P, 2, OUTF], U32, name="w_codes", align_bytes=64)
-        w_scl = const.tile([P, 2, OUTF], U8, name="w_scl", align_bytes=64)
-
-        def weight_regroup(c):
-            nc.vector.tensor_copy(
-                out=w_grp[:, c].rearrange("p (a i) t -> p a t i", i=4),
-                in_=w_raw[:, c].rearrange("p t (a i) -> p a t i", i=4),
-            )
-
-        weight_regroup(0)
-        degree_recip(0)
-        for r in range(2):
+        degree_spread(0)
+        degree_resort(0)
+        bias_matmul(CLOCK_REPEATS)
+        degree_root(0)
+        weight_group(0)
+        degree_reciprocal(0)
+        for r in range(LEAD):
             scale_rows(r)
-            transposes(r, 0)
-            bias_matmul(WARM)
-            transposes(r, 1)
-            regroup(r, 0)
-            regroup(r, 1)
+            transpose_slice(r, 0)
+            bias_matmul(CLOCK_REPEATS)
+            transpose_slice(r, 1)
+            group_slice(r, 0)
+            group_slice(r, 1)
             if r == 0:
-                weight_regroup(1)
+                weight_group(1)
         nc.vector.quantize_mx(
-            out=w_codes[:].rearrange("p c o -> p (c o)").bitcast(FP8X4),
-            scales=w_scl[:].rearrange("p c o -> p (c o)"),
-            in_=w_grp[:].rearrange("p c o t -> p (c o t)"),
+            out=w_words[:].rearrange("p c o -> p (c o)").bitcast(FP8X4),
+            scales=w_scales[:].rearrange("p c o -> p (c o)"),
+            in_=w_grouped[:].rearrange("p c o t -> p (c o t)"),
         )
-        col_sums(1, 0)
-        col_sums(1, 1)
-        bias_matmul(WARM)
+        column_sums(1, 0)
+        column_sums(1, 1)
+        bias_matmul(CLOCK_REPEATS)
+
+        def sums_due(r, s):
+            if r == 0:
+                return [(1, PAIR + s)]
+            g, k = divmod(r + LEAD, ROUNDS_PER_GRAPH)
+            if k < LEAD and g + 1 < GRAPHS:
+                return [(g + 1, PAIR * k + s)]
+            return []
 
         for r in range(ROUNDS + 1):
-            nxt = r // 4 + 1
-            degrees_now = r % 4 == 1 and nxt < GRAPHS
-            if r + 2 < ROUNDS:
-                scale_rows(r + 2)
-                if r + 2 == 3:
+            ahead = r + LEAD
+            behind = r - 1
+            next_graph = r // ROUNDS_PER_GRAPH + 1
+            degrees_now = r % ROUNDS_PER_GRAPH == 1 and next_graph < GRAPHS
+
+            if ahead < ROUNDS:
+                scale_rows(ahead)
+                if ahead == ROUNDS_PER_GRAPH - 1:
                     load_x(3, 0, 4)
                     load_x(3, 4, 8)
             if r < ROUNDS:
                 quantise(r)
             if degrees_now:
-                degree_v(nxt)
-            if r + 2 < ROUNDS:
-                transposes(r + 2, 0)
-                transposes(r + 2, 1)
-            if r < ROUNDS:
-                products(r, 0)
-                products(r, 1)
-            for s in range(2):
-                for g, c in SUMS_AT.get((r, s), []):
-                    col_sums(g, c)
+                degree_spread(next_graph)
+            for s in range(PAIR):
+                if ahead < ROUNDS:
+                    transpose_slice(ahead, s)
+                if r < ROUNDS:
+                    multiply_slice(r, s)
+                for g, c in sums_due(r, s):
+                    column_sums(g, c)
+                if degrees_now and s == 0:
+                    degree_resort(next_graph)
+            if behind >= 0:
+                add_bias(behind)
+            last_copies = ahead == ROUNDS - 1
+            if ahead < ROUNDS:
+                group_slice(ahead, 0)
             if degrees_now:
-                degree_pe(nxt)
-            if r >= 1:
-                add_bias(r - 1)
-            if r + 2 < ROUNDS:
-                regroup(r + 2, 0)
+                degree_root(next_graph)
+            if behind >= 0 and not last_copies:
+                relu_slice(behind, 0, "scalar")
+            if ahead < ROUNDS:
+                group_slice(ahead, 1)
+            if behind >= 0 and last_copies:
+                relu_slice(behind, 0, "scalar")
+            if behind == ROUNDS - 1:
+                store(behind, 0, 1)
+                relu_slice(behind, 1, "vector")
+                store(behind, 1, 2)
+            elif behind >= 0:
+                relu_slice(behind, 1, "scalar" if ahead >= ROUNDS else "vector")
+                store(behind, 0, PAIR)
             if degrees_now:
-                degree_sqrt(nxt)
-            if r >= 1 and r + 2 != ROUNDS - 1:
-                relu_scalar(r - 1)
-            if r + 2 < ROUNDS:
-                regroup(r + 2, 1)
-            if r >= 1 and r + 2 == ROUNDS - 1:
-                relu_scalar(r - 1)
-            if r >= 1:
-                relu_vector_store(r - 1)
-            if degrees_now:
-                degree_recip(nxt)
+                degree_reciprocal(next_graph)

@@ -29,7 +29,6 @@ CHUNKS = 4
 CHUNK_ROWS = 2
 SUM_COLS = 16
 SPREAD = P // SLICES
-CLOCK_REPEATS = 2
 RESIDENT = 3
 RESULT_BUFS = 12
 LOOP = 1.0
@@ -180,12 +179,6 @@ def tile_gcn_t_kernel(tc, x, mask, weight, bias, out):
             inv_sqrt_d[g] = small.tile([P, SLICES], F32, name="inv_sqrt_d%d" % g, tag="inv_sqrt_d")
             nc.vector.reciprocal(out=inv_sqrt_d[g][:], in_=root_tiles[g][:])
 
-        def bias_matmul(times):
-            for repeat in range(times):
-                nc.tensor.matmul(
-                    out=bias_bank[:], lhsT=ones_b[:], rhs=bias_row[:], start=True, stop=True
-                )
-
         def weight_group(c):
             nc.vector.tensor_copy(
                 out=w_grouped[:, c].rearrange("p (a i) t -> p a t i", i=4),
@@ -300,23 +293,20 @@ def tile_gcn_t_kernel(tc, x, mask, weight, bias, out):
 
         column_sums(0, 0)
         column_sums(0, 1)
-        bias_matmul(1)
+        nc.tensor.matmul(out=bias_bank[:], lhsT=ones_b[:], rhs=bias_row[:], start=True, stop=True)
         nc.scalar.copy(out=bias_all[:], in_=bias_bank[:])
         column_sums(0, 2)
         column_sums(0, 3)
-        bias_matmul(CLOCK_REPEATS)
         load_mask(3, 0, 4)
         self_loops(3)
         degree_spread(0)
         degree_resort(0)
-        bias_matmul(CLOCK_REPEATS)
         degree_root(0)
         weight_group(0)
         degree_reciprocal(0)
         for r in range(LEAD):
             scale_rows(r)
             transpose_slice(r, 0)
-            bias_matmul(CLOCK_REPEATS)
             transpose_slice(r, 1)
             group_slice(r, 0)
             group_slice(r, 1)
@@ -329,7 +319,6 @@ def tile_gcn_t_kernel(tc, x, mask, weight, bias, out):
         )
         column_sums(1, 0)
         column_sums(1, 1)
-        bias_matmul(CLOCK_REPEATS)
 
         def sums_due(r, s):
             if r == 0:

from contextlib import ExitStack

import concourse.mybir as mybir
from concourse.masks import make_identity

FP8X4 = mybir.dt.float8_e4m3fn_x4
BF16 = mybir.dt.bfloat16
F32 = mybir.dt.float32
U32 = mybir.dt.uint32
U8 = mybir.dt.uint8
ALU = mybir.AluOpType
ACT = mybir.ActivationFunctionType
AX = mybir.AxisListType

P = 128
PACK = 4
GRAPHS = 4
NODES = 1024
FEAT = 1024
OUTF = 512
PASSES = FEAT // (P * PACK)
BLOCKS = FEAT // P
SLICES = NODES // P
PAIR = 2
ROUNDS_PER_GRAPH = SLICES // PAIR
ROUNDS = GRAPHS * ROUNDS_PER_GRAPH
LEAD = 2
CHUNKS = 4
CHUNK_ROWS = 2
SUM_COLS = 16
SPREAD = P // SLICES
RESIDENT = 3
RESULT_BUFS = 12
LOOP = 1.0
FLOPS = 2 * GRAPHS * NODES * FEAT * OUTF


def tile_gcn_t_kernel(tc, x, mask, weight, bias, out):
    nc = tc.nc
    x_view = x.rearrange("a b (p t) k -> (a b) p t k", t=SLICES)
    out_view = out.rearrange("a b (p t) o -> (a b) p t o", t=SLICES)
    mask_view = mask.rearrange("a b (c p t) i -> (a b) p c t i", c=CHUNKS, p=P, t=CHUNK_ROWS)
    weight_view = weight.rearrange("(c t p) o -> p c t o", c=PASSES, t=PACK, p=P)
    bias_view = bias.rearrange("(r n) -> r n", r=1)

    with ExitStack() as ctx:
        const = ctx.enter_context(tc.tile_pool(name="const", bufs=1))
        mask_pool = ctx.enter_context(tc.tile_pool(name="mask_pool", bufs=RESIDENT))
        x_pool = ctx.enter_context(tc.tile_pool(name="x_pool", bufs=RESIDENT))
        work = ctx.enter_context(tc.tile_pool(name="work", bufs=LEAD + 1))
        small = ctx.enter_context(tc.tile_pool(name="small", bufs=2))
        result_pool = ctx.enter_context(tc.tile_pool(name="result_pool", bufs=RESULT_BUFS))
        psum_t = ctx.enter_context(tc.psum_pool(name="psum_t", bufs=3))
        psum_o = ctx.enter_context(tc.psum_pool(name="psum_o", bufs=4))
        psum_d = ctx.enter_context(tc.psum_pool(name="psum_d", bufs=1))
        ctx.enter_context(tc.manual_schedule())

        mask_tiles = {}
        x_tiles = {}
        sum_banks = {}
        spread_tiles = {}
        root_tiles = {}
        inv_sqrt_d = {}
        scaled = {}
        flipped = {}
        grouped = {}
        packed = {}
        products = {}
        results = {}

        ident_f = const.tile([P, P], F32, name="ident_f")
        make_identity(nc, ident_f[:])
        one_col = const.tile([P, 1], F32, name="one_col")
        nc.vector.memset(one_col[:], 1.0)
        bias_row = const.tile([P, OUTF], BF16, name="bias_row")
        nc.vector.memset(bias_row[:], 0.0)
        first_sqrt = const.tile([P, 1], F32, name="first_sqrt")
        nc.scalar.sqrt(out=first_sqrt[:], in_=one_col[:])
        ones_b = const.tile([P, P], BF16, name="ones_b")
        nc.vector.memset(ones_b[:], 1.0)
        ident_b = const.tile([P, P], BF16, name="ident_b")
        nc.vector.tensor_copy(out=ident_b[:], in_=ident_f[:])
        row_in_group = const.tile([P, SLICES], F32, name="row_in_group")
        nc.vector.tensor_reduce(
            out=row_in_group[:],
            in_=ident_f[:].rearrange("p (q t) -> p t q", t=SLICES),
            axis=AX.X,
            op=ALU.add,
        )
        group_of_row = const.tile([P, SPREAD], F32, name="group_of_row")
        nc.vector.tensor_reduce(
            out=group_of_row[:],
            in_=ident_f[:].rearrange("p (q t) -> p q t", t=SLICES),
            axis=AX.X,
            op=ALU.add,
        )
        bias_all = const.tile([P, OUTF], F32, name="bias_all")
        w_raw = const.tile([P, PASSES, PACK, OUTF], BF16, name="w_raw")
        w_grouped = const.tile([P, PASSES, OUTF, PACK], BF16, name="w_grouped", align_bytes=64)
        w_words = const.tile([P, PASSES, OUTF], U32, name="w_words", align_bytes=64)
        w_scales = const.tile([P, PASSES, OUTF], U8, name="w_scales", align_bytes=64)
        bias_bank = psum_o.tile([P, OUTF], F32, name="bias_bank", tag="o")

        def load_mask(g, first_chunk, end_chunk):
            if g not in mask_tiles:
                mask_tiles[g] = mask_pool.tile(
                    [P, CHUNKS, CHUNK_ROWS, NODES], BF16, name="mask%d" % g, tag="mask"
                )
            for c in range(first_chunk, end_chunk):
                nc.sync.dma_start(out=mask_tiles[g][:, c], in_=mask_view[g][:, c])

        def load_x(g, first_slice, end_slice):
            if g not in x_tiles:
                x_tiles[g] = x_pool.tile([P, SLICES, FEAT], BF16, name="x%d" % g, tag="x")
            rows = slice(first_slice, end_slice)
            nc.sync.dma_start(out=x_tiles[g][:, rows, :], in_=x_view[g][:, rows, :])

        def self_loops(g):
            width = P * CHUNK_ROWS
            for c in range(CHUNKS):
                for t in range(CHUNK_ROWS):
                    region = mask_tiles[g][:, c, t, c * width : (c + 1) * width]
                    nc.gpsimd.affine_select(
                        out=region,
                        in_=region,
                        pattern=[[-1, width]],
                        compare_op=ALU.not_equal,
                        fill=LOOP,
                        base=t,
                        channel_multiplier=CHUNK_ROWS,
                    )

        def column_sums(g, c):
            if c == 0:
                sum_banks[g] = psum_d.tile(
                    [P, CHUNKS, BLOCKS, SUM_COLS], F32, name="sums%d" % g, tag="d"
                )
            with_diagonal = [CHUNK_ROWS * c + t for t in range(CHUNK_ROWS)]
            for b in [b for b in range(BLOCKS) if b not in with_diagonal] + with_diagonal:
                for t in range(CHUNK_ROWS):
                    nc.tensor.matmul(
                        out=sum_banks[g][:, c, b, :],
                        lhsT=mask_tiles[g][:, c, t, b * P : (b + 1) * P],
                        rhs=ones_b[:, 0:SUM_COLS],
                        start=(t == 0),
                        stop=(t == CHUNK_ROWS - 1),
                    )

        def degree_spread(g):
            d_block = small.tile([P, BLOCKS], F32, name="d_block%d" % g, tag="d_block")
            nc.vector.tensor_reduce(
                out=d_block[:],
                in_=sum_banks[g][:].rearrange("p c b n -> p b c n")[:, :, :, 0],
                axis=AX.X,
                op=ALU.add,
            )
            spread_tiles[g] = small.tile([P, BLOCKS, SPREAD], F32, name="spread%d" % g, tag="spread")
            nc.vector.tensor_tensor(
                out=spread_tiles[g][:],
                in0=d_block[:].unsqueeze(2).to_broadcast([P, BLOCKS, SPREAD]),
                in1=group_of_row[:].unsqueeze(1).to_broadcast([P, BLOCKS, SPREAD]),
                op=ALU.mult,
            )

        def degree_resort(g):
            nc.tensor.matmul(
                out=sum_banks[g][:, 0, 0, 0:SLICES],
                lhsT=spread_tiles[g][:].rearrange("p b q -> p (b q)"),
                rhs=row_in_group[:],
                start=True,
                stop=True,
            )

        def degree_root(g):
            root_tiles[g] = small.tile([P, SLICES], F32, name="root%d" % g, tag="root")
            nc.scalar.sqrt(out=root_tiles[g][:], in_=sum_banks[g][:, 0, 0, 0:SLICES])

        def degree_reciprocal(g):
            inv_sqrt_d[g] = small.tile([P, SLICES], F32, name="inv_sqrt_d%d" % g, tag="inv_sqrt_d")
            nc.vector.reciprocal(out=inv_sqrt_d[g][:], in_=root_tiles[g][:])

        def weight_group(c):
            nc.vector.tensor_copy(
                out=w_grouped[:, c].rearrange("p (a i) t -> p a t i", i=4),
                in_=w_raw[:, c].rearrange("p t (a i) -> p a t i", i=4),
            )

        def scale_rows(r):
            g, q = divmod(r, ROUNDS_PER_GRAPH)
            scaled[r] = work.tile([P, PAIR, FEAT], BF16, name="scaled%d" % r, tag="scaled")
            for s in range(PAIR):
                t = PAIR * q + s
                nc.vector.tensor_scalar(
                    out=scaled[r][:, s, :],
                    in0=x_tiles[g][:, t, :],
                    scalar1=inv_sqrt_d[g][:, t : t + 1],
                    scalar2=None,
                    op0=ALU.mult,
                )

        def transpose_slice(r, s):
            bank = psum_t.tile([P, BLOCKS, P], BF16, name="flipped%d_%d" % (r, s), tag="t")
            flipped[(r, s)] = bank
            for b in range(BLOCKS):
                nc.tensor.transpose(bank[:, b, :], scaled[r][:, s, b * P : (b + 1) * P], ident_b[:])

        def group_slice(r, s):
            if s == 0:
                grouped[r] = work.tile(
                    [P, PAIR, PASSES, P, PACK], BF16, name="grouped%d" % r, tag="grouped", align_bytes=64
                )
            nc.scalar.copy(
                out=grouped[r][:, s],
                in_=flipped[(r, s)][:].rearrange("p (c t) i -> p c i t", c=PASSES),
            )

        def quantise(r):
            width = PASSES * P
            words = work.tile([P, PAIR * width], U32, name="words%d" % r, tag="words", align_bytes=64)
            scales = work.tile([P, PAIR * width], U8, name="scales%d" % r, tag="scales", align_bytes=64)
            packed[r] = (words, scales)
            if r == ROUNDS - 1:
                for s in range(PAIR):
                    cols = slice(s * width, (s + 1) * width)
                    nc.vector.quantize_mx(
                        out=words[:, cols].bitcast(FP8X4),
                        scales=scales[:, cols],
                        in_=grouped[r][:, s].rearrange("p c i t -> p (c i t)"),
                    )
            else:
                nc.vector.quantize_mx(
                    out=words[:].bitcast(FP8X4),
                    scales=scales[:],
                    in_=grouped[r][:].rearrange("p s c i t -> p (s c i t)"),
                )

        def multiply_slice(r, s):
            words, scales = packed[r]
            bank = psum_o.tile([P, OUTF], F32, name="product%d_%d" % (r, s), tag="o")
            products[(r, s)] = bank
            for c in range(PASSES):
                cols = slice((PASSES * s + c) * P, (PASSES * s + c + 1) * P)
                nc.tensor.matmul_mx(
                    out=bank[:],
                    lhsT=words[:, cols].bitcast(FP8X4),
                    lhsT_scale=scales[:, cols],
                    rhs=w_words[:, c, :].bitcast(FP8X4),
                    rhs_scale=w_scales[:, c, :],
                    start=(c == 0),
                    stop=(c == PASSES - 1),
                )

        def add_bias(r):
            results[r] = result_pool.tile([P, PAIR, OUTF], F32, name="result%d" % r, tag="result")
            for s in range(PAIR):
                nc.vector.tensor_tensor(
                    out=results[r][:, s, :], in0=products[(r, s)][:], in1=bias_all[:], op=ALU.add
                )

        def relu_slice(r, s, engine):
            part = results[r][:, s, :]
            if engine == "scalar":
                nc.scalar.activation(out=part, in_=part, func=ACT.Relu)
            else:
                nc.vector.tensor_scalar_max(out=part, in0=part, scalar1=0.0)

        def store(r, first_slice, end_slice):
            g, q = divmod(r, ROUNDS_PER_GRAPH)
            nc.sync.dma_start(
                out=out_view[g][:, PAIR * q + first_slice : PAIR * q + end_slice, :],
                in_=results[r][:, first_slice:end_slice, :],
            )

        load_mask(0, 0, 2)
        nc.sync.dma_start(out=bias_row[0:1, :], in_=bias_view)
        load_mask(0, 2, 4)
        nc.sync.dma_start(out=w_raw[:], in_=weight_view)
        load_x(0, 0, 2)
        load_x(0, 2, 4)
        load_mask(1, 0, 2)
        load_x(0, 4, 6)
        load_mask(1, 2, 4)
        load_x(0, 6, 8)
        load_x(1, 0, 2)
        load_x(1, 2, 4)
        load_mask(2, 0, 2)
        load_x(1, 4, 8)
        load_mask(2, 2, 4)
        load_x(2, 0, 4)
        load_x(2, 4, 8)
        for g in range(RESIDENT):
            self_loops(g)

        column_sums(0, 0)
        column_sums(0, 1)
        nc.tensor.matmul(out=bias_bank[:], lhsT=ones_b[:], rhs=bias_row[:], start=True, stop=True)
        nc.scalar.copy(out=bias_all[:], in_=bias_bank[:])
        column_sums(0, 2)
        column_sums(0, 3)
        load_mask(3, 0, 4)
        self_loops(3)
        degree_spread(0)
        degree_resort(0)
        degree_root(0)
        weight_group(0)
        degree_reciprocal(0)
        for r in range(LEAD):
            scale_rows(r)
            transpose_slice(r, 0)
            transpose_slice(r, 1)
            group_slice(r, 0)
            group_slice(r, 1)
            if r == 0:
                weight_group(1)
        nc.vector.quantize_mx(
            out=w_words[:].rearrange("p c o -> p (c o)").bitcast(FP8X4),
            scales=w_scales[:].rearrange("p c o -> p (c o)"),
            in_=w_grouped[:].rearrange("p c o t -> p (c o t)"),
        )
        column_sums(1, 0)
        column_sums(1, 1)

        def sums_due(r, s):
            if r == 0:
                return [(1, PAIR + s)]
            g, k = divmod(r + LEAD, ROUNDS_PER_GRAPH)
            if k < LEAD and g + 1 < GRAPHS:
                return [(g + 1, PAIR * k + s)]
            return []

        for r in range(ROUNDS + 1):
            ahead = r + LEAD
            behind = r - 1
            next_graph = r // ROUNDS_PER_GRAPH + 1
            degrees_now = r % ROUNDS_PER_GRAPH == 1 and next_graph < GRAPHS

            if ahead < ROUNDS:
                scale_rows(ahead)
                if ahead == ROUNDS_PER_GRAPH - 1:
                    load_x(3, 0, 4)
                    load_x(3, 4, 8)
            if r < ROUNDS:
                quantise(r)
            if degrees_now:
                degree_spread(next_graph)
            for s in range(PAIR):
                if ahead < ROUNDS:
                    transpose_slice(ahead, s)
                if r < ROUNDS:
                    multiply_slice(r, s)
                for g, c in sums_due(r, s):
                    column_sums(g, c)
                if degrees_now and s == 0:
                    degree_resort(next_graph)
            if behind >= 0:
                add_bias(behind)
            last_copies = ahead == ROUNDS - 1
            if ahead < ROUNDS:
                group_slice(ahead, 0)
            if degrees_now:
                degree_root(next_graph)
            if behind >= 0 and not last_copies:
                relu_slice(behind, 0, "scalar")
            if ahead < ROUNDS:
                group_slice(ahead, 1)
            if behind >= 0 and last_copies:
                relu_slice(behind, 0, "scalar")
            if behind == ROUNDS - 1:
                store(behind, 0, 1)
                relu_slice(behind, 1, "vector")
                store(behind, 1, 2)
            elif behind >= 0:
                relu_slice(behind, 1, "scalar" if ahead >= ROUNDS else "vector")
                store(behind, 0, PAIR)
            if degrees_now:
                degree_reciprocal(next_graph)
